import numpy as np
import ml_dtypes

BF16 = ml_dtypes.bfloat16


def bf(x):
    return np.asarray(x, np.float32).astype(BF16)


def f32(x):
    return np.asarray(x, np.float32)


def f64(x):
    return np.asarray(x).astype(np.float64)


def striped(idx):
    return np.tile(idx.reshape(-1, 16).T, (8, 1))


C, S, B, T, N = 768, 2048, 4, 256, 1024
BASE = 10000.0


def positions(t_len, dim):
    i = np.arange(dim)
    exponent = (2 * (i // 2)).astype(np.float32) / np.float32(dim)
    t = np.arange(t_len, dtype=np.float32)[None, :]
    angle = t / np.power(np.float32(BASE), exponent)[:, None]
    return np.where((i % 2 == 0)[:, None], np.sin(angle), np.cos(angle))


def setup_inputs():
    return {"embedding": f32(np.random.standard_normal((C, S))), "pos": f32(positions(T, C)), "offs": striped(np.random.permutation(np.tile(np.arange(S), 2))[:N])}


def reference(embedding, pos, offs):
    idx = offs[:16].T.reshape(-1)
    return f64(embedding)[:, idx] + np.tile(f64(pos), (1, B))

@@ -1,0 +1,33 @@
+import concourse.mybir as mybir
+
+P = 128
+C, S = 768, 2048
+T, N = 256, 1024
+BLOCKS = C // P
+SEQUENCES = N // T
+SEQ_COLS = T // 16
+F32, U16 = mybir.dt.float32, mybir.dt.uint16
+ADD = mybir.AluOpType.add
+
+
+def tile_microgpttorch_kernel(tc, embedding, pos, offs, out):
+    nc = tc.nc
+    with (
+        tc.tile_pool(name="held", bufs=1) as held,
+        tc.tile_pool(name="blocks", bufs=BLOCKS) as blocks,
+    ):
+        offsets = held.tile([P, N // 16], U16, name="offsets")
+        nc.sync.dma_start(offsets[:], offs)
+
+        for b in range(BLOCKS):
+            rows = slice(b * P, (b + 1) * P)
+            table = blocks.tile([P, S], F32, name="table")
+            nc.sync.dma_start(table[:], embedding[rows, :])
+            code = blocks.tile([P, T], F32, name="code")
+            nc.sync.dma_start(code[:], pos[rows, :])
+
+            summed = blocks.tile([P, N], F32, name="summed")
+            for s in range(SEQUENCES):
+                picked = table[:].indirect(offsets[:, s * SEQ_COLS : (s + 1) * SEQ_COLS])
+                nc.vector.tensor_tensor(summed[:, s * T : (s + 1) * T], picked, code[:], ADD)
+            nc.scalar.dma_start(out[rows, :], summed[:])

@@ -19,15 +19,20 @@ def tile_microgpttorch_kernel(tc, embedding, pos, offs, out):
         offsets = held.tile([P, N // 16], U16, name="offsets")
         nc.sync.dma_start(offsets[:], offs)
 
+        tables, codes = [], []
         for b in range(BLOCKS):
             rows = slice(b * P, (b + 1) * P)
             table = blocks.tile([P, S], F32, name="table")
             nc.sync.dma_start(table[:], embedding[rows, :])
+            tables.append(table)
             code = blocks.tile([P, T], F32, name="code")
             nc.sync.dma_start(code[:], pos[rows, :])
+            codes.append(code)
 
+        for b in range(BLOCKS):
+            rows = slice(b * P, (b + 1) * P)
             summed = blocks.tile([P, N], F32, name="summed")
             for s in range(SEQUENCES):
-                picked = table[:].indirect(offsets[:, s * SEQ_COLS : (s + 1) * SEQ_COLS])
-                nc.vector.tensor_tensor(summed[:, s * T : (s + 1) * T], picked, code[:], ADD)
-            nc.scalar.dma_start(out[rows, :], summed[:])
+                picked = tables[b][:].indirect(offsets[:, s * SEQ_COLS : (s + 1) * SEQ_COLS])
+                nc.vector.tensor_tensor(summed[:, s * T : (s + 1) * T], picked, codes[b][:], ADD)
+            nc.sync.dma_start(out[rows, :], summed[:])

@@ -5,7 +5,6 @@ C, S = 768, 2048
 T, N = 256, 1024
 BLOCKS = C // P
 SEQUENCES = N // T
-SEQ_COLS = T // 16
 F32, U16 = mybir.dt.float32, mybir.dt.uint16
 ADD = mybir.AluOpType.add
 
@@ -22,17 +21,18 @@ def tile_microgpttorch_kernel(tc, embedding, pos, offs, out):
         tables, codes = [], []
         for b in range(BLOCKS):
             rows = slice(b * P, (b + 1) * P)
-            table = blocks.tile([P, S], F32, name="table")
-            nc.sync.dma_start(table[:], embedding[rows, :])
-            tables.append(table)
             code = blocks.tile([P, T], F32, name="code")
             nc.sync.dma_start(code[:], pos[rows, :])
             codes.append(code)
+            table = blocks.tile([P, S], F32, name="table")
+            nc.sync.dma_start(table[:], embedding[rows, :])
+            tables.append(table)
 
         for b in range(BLOCKS):
             rows = slice(b * P, (b + 1) * P)
+            repeated = blocks.tile([P, SEQUENCES, T], F32, name="repeated")
+            nc.scalar.copy(repeated[:], codes[b][:].unsqueeze(1).to_broadcast([P, SEQUENCES, T]))
             summed = blocks.tile([P, N], F32, name="summed")
-            for s in range(SEQUENCES):
-                picked = tables[b][:].indirect(offsets[:, s * SEQ_COLS : (s + 1) * SEQ_COLS])
-                nc.vector.tensor_tensor(summed[:, s * T : (s + 1) * T], picked, codes[b][:], ADD)
+            picked = tables[b][:].indirect(offsets[:])
+            nc.vector.tensor_tensor(summed[:], picked, repeated[:].rearrange("p s t -> p (s t)"), ADD)
             nc.sync.dma_start(out[rows, :], summed[:])

@@ -5,12 +5,17 @@ C, S = 768, 2048
 T, N = 256, 1024
 BLOCKS = C // P
 SEQUENCES = N // T
+STORE_GROUPS = (3, 2, 1)
 F32, U16 = mybir.dt.float32, mybir.dt.uint16
 ADD = mybir.AluOpType.add
 
 
 def tile_microgpttorch_kernel(tc, embedding, pos, offs, out):
     nc = tc.nc
+    assert sum(STORE_GROUPS) == BLOCKS
+    embedding_blocks = embedding.rearrange("(p b) s -> p b s", b=BLOCKS)
+    pos_rows = pos.rearrange("(p b) t -> p (b t)", b=BLOCKS)
+    out_rows = out.rearrange("(p b) n -> p (b n)", b=BLOCKS)
     with (
         tc.tile_pool(name="held", bufs=1) as held,
         tc.tile_pool(name="blocks", bufs=BLOCKS) as blocks,
@@ -18,21 +23,26 @@ def tile_microgpttorch_kernel(tc, embedding, pos, offs, out):
         offsets = held.tile([P, N // 16], U16, name="offsets")
         nc.sync.dma_start(offsets[:], offs)
 
-        tables, codes = [], []
+        codes = held.tile([P, BLOCKS * T], F32, name="codes")
+        nc.sync.dma_start(codes[:], pos_rows)
+
+        tables = []
         for b in range(BLOCKS):
-            rows = slice(b * P, (b + 1) * P)
-            code = blocks.tile([P, T], F32, name="code")
-            nc.sync.dma_start(code[:], pos[rows, :])
-            codes.append(code)
             table = blocks.tile([P, S], F32, name="table")
-            nc.sync.dma_start(table[:], embedding[rows, :])
+            nc.sync.dma_start(table[:], embedding_blocks[:, b, :])
             tables.append(table)
 
-        for b in range(BLOCKS):
-            rows = slice(b * P, (b + 1) * P)
-            repeated = blocks.tile([P, SEQUENCES, T], F32, name="repeated")
-            nc.scalar.copy(repeated[:], codes[b][:].unsqueeze(1).to_broadcast([P, SEQUENCES, T]))
-            summed = blocks.tile([P, N], F32, name="summed")
-            picked = tables[b][:].indirect(offsets[:])
-            nc.vector.tensor_tensor(summed[:], picked, repeated[:].rearrange("p s t -> p (s t)"), ADD)
-            nc.sync.dma_start(out[rows, :], summed[:])
+        first = 0
+        for g, size in enumerate(STORE_GROUPS):
+            summed = held.tile([P, size * N], F32, name="summed%d" % g)
+            for k in range(size):
+                b = first + k
+                repeated = blocks.tile([P, SEQUENCES, T], F32, name="repeated")
+                code = codes[:, b * T : (b + 1) * T]
+                nc.scalar.copy(repeated[:], code.unsqueeze(1).to_broadcast([P, SEQUENCES, T]))
+                picked = tables[b][:].indirect(offsets[:])
+                nc.vector.tensor_tensor(
+                    summed[:, k * N : (k + 1) * N], picked, repeated[:].rearrange("p s t -> p (s t)"), ADD
+                )
+            nc.sync.dma_start(out_rows[:, first * N : (first + size) * N], summed[:])
+            first += size

@@ -5,6 +5,7 @@ C, S = 768, 2048
 T, N = 256, 1024
 BLOCKS = C // P
 SEQUENCES = N // T
+CODE_BLOCKS = 2
 STORE_GROUPS = (3, 2, 1)
 F32, U16 = mybir.dt.float32, mybir.dt.uint16
 ADD = mybir.AluOpType.add
@@ -12,7 +13,7 @@ ADD = mybir.AluOpType.add
 
 def tile_microgpttorch_kernel(tc, embedding, pos, offs, out):
     nc = tc.nc
-    assert sum(STORE_GROUPS) == BLOCKS
+    assert sum(STORE_GROUPS) == BLOCKS and BLOCKS % CODE_BLOCKS == 0
     embedding_blocks = embedding.rearrange("(p b) s -> p b s", b=BLOCKS)
     pos_rows = pos.rearrange("(p b) t -> p (b t)", b=BLOCKS)
     out_rows = out.rearrange("(p b) n -> p (b n)", b=BLOCKS)
@@ -23,11 +24,12 @@ def tile_microgpttorch_kernel(tc, embedding, pos, offs, out):
         offsets = held.tile([P, N // 16], U16, name="offsets")
         nc.sync.dma_start(offsets[:], offs)
 
-        codes = held.tile([P, BLOCKS * T], F32, name="codes")
-        nc.sync.dma_start(codes[:], pos_rows)
-
-        tables = []
+        tables, codes = [], []
         for b in range(BLOCKS):
+            if b % CODE_BLOCKS == 0:
+                pair = blocks.tile([P, CODE_BLOCKS * T], F32, name="pair")
+                nc.sync.dma_start(pair[:], pos_rows[:, b * T : (b + CODE_BLOCKS) * T])
+                codes.extend(pair[:, k * T : (k + 1) * T] for k in range(CODE_BLOCKS))
             table = blocks.tile([P, S], F32, name="table")
             nc.sync.dma_start(table[:], embedding_blocks[:, b, :])
             tables.append(table)
@@ -38,8 +40,7 @@ def tile_microgpttorch_kernel(tc, embedding, pos, offs, out):
             for k in range(size):
                 b = first + k
                 repeated = blocks.tile([P, SEQUENCES, T], F32, name="repeated")
-                code = codes[:, b * T : (b + 1) * T]
-                nc.scalar.copy(repeated[:], code.unsqueeze(1).to_broadcast([P, SEQUENCES, T]))
+                nc.scalar.copy(repeated[:], codes[b].unsqueeze(1).to_broadcast([P, SEQUENCES, T]))
                 picked = tables[b][:].indirect(offsets[:])
                 nc.vector.tensor_tensor(
                     summed[:, k * N : (k + 1) * N], picked, repeated[:].rearrange("p s t -> p (s t)"), ADD

@@ -5,6 +5,7 @@ C, S = 768, 2048
 T, N = 256, 1024
 BLOCKS = C // P
 SEQUENCES = N // T
+SEQ_COLS = T // 16
 CODE_BLOCKS = 2
 STORE_GROUPS = (3, 2, 1)
 F32, U16 = mybir.dt.float32, mybir.dt.uint16
@@ -39,11 +40,10 @@ def tile_microgpttorch_kernel(tc, embedding, pos, offs, out):
             summed = held.tile([P, size * N], F32, name="summed%d" % g)
             for k in range(size):
                 b = first + k
-                repeated = blocks.tile([P, SEQUENCES, T], F32, name="repeated")
-                nc.scalar.copy(repeated[:], codes[b].unsqueeze(1).to_broadcast([P, SEQUENCES, T]))
-                picked = tables[b][:].indirect(offsets[:])
-                nc.vector.tensor_tensor(
-                    summed[:, k * N : (k + 1) * N], picked, repeated[:].rearrange("p s t -> p (s t)"), ADD
-                )
+                for s in range(SEQUENCES):
+                    picked = tables[b][:].indirect(offsets[:, s * SEQ_COLS : (s + 1) * SEQ_COLS])
+                    nc.vector.tensor_tensor(
+                        summed[:, k * N + s * T : k * N + (s + 1) * T], picked, codes[b], ADD
+                    )
             nc.sync.dma_start(out_rows[:, first * N : (first + size) * N], summed[:])
             first += size

@@ -7,14 +7,14 @@ BLOCKS = C // P
 SEQUENCES = N // T
 SEQ_COLS = T // 16
 CODE_BLOCKS = 2
-STORE_GROUPS = (3, 2, 1)
+STORE_SEQUENCES = (12, 8, 2, 2)
 F32, U16 = mybir.dt.float32, mybir.dt.uint16
 ADD = mybir.AluOpType.add
 
 
 def tile_microgpttorch_kernel(tc, embedding, pos, offs, out):
     nc = tc.nc
-    assert sum(STORE_GROUPS) == BLOCKS and BLOCKS % CODE_BLOCKS == 0
+    assert sum(STORE_SEQUENCES) == BLOCKS * SEQUENCES and BLOCKS % CODE_BLOCKS == 0
     embedding_blocks = embedding.rearrange("(p b) s -> p b s", b=BLOCKS)
     pos_rows = pos.rearrange("(p b) t -> p (b t)", b=BLOCKS)
     out_rows = out.rearrange("(p b) n -> p (b n)", b=BLOCKS)
@@ -36,14 +36,11 @@ def tile_microgpttorch_kernel(tc, embedding, pos, offs, out):
             tables.append(table)
 
         first = 0
-        for g, size in enumerate(STORE_GROUPS):
-            summed = held.tile([P, size * N], F32, name="summed%d" % g)
+        for g, size in enumerate(STORE_SEQUENCES):
+            summed = held.tile([P, size * T], F32, name="summed%d" % g)
             for k in range(size):
-                b = first + k
-                for s in range(SEQUENCES):
-                    picked = tables[b][:].indirect(offsets[:, s * SEQ_COLS : (s + 1) * SEQ_COLS])
-                    nc.vector.tensor_tensor(
-                        summed[:, k * N + s * T : k * N + (s + 1) * T], picked, codes[b], ADD
-                    )
-            nc.sync.dma_start(out_rows[:, first * N : (first + size) * N], summed[:])
+                b, s = divmod(first + k, SEQUENCES)
+                picked = tables[b][:].indirect(offsets[:, s * SEQ_COLS : (s + 1) * SEQ_COLS])
+                nc.vector.tensor_tensor(summed[:, k * T : (k + 1) * T], picked, codes[b], ADD)
+            nc.sync.dma_start(out_rows[:, first * T : (first + size) * T], summed[:])
             first += size

@@ -22,18 +22,18 @@ def tile_microgpttorch_kernel(tc, embedding, pos, offs, out):
         tc.tile_pool(name="held", bufs=1) as held,
         tc.tile_pool(name="blocks", bufs=BLOCKS) as blocks,
     ):
-        offsets = held.tile([P, N // 16], U16, name="offsets")
-        nc.sync.dma_start(offsets[:], offs)
-
         tables, codes = [], []
         for b in range(BLOCKS):
+            table = blocks.tile([P, S], F32, name="table")
+            nc.sync.dma_start(table[:], embedding_blocks[:, b, :])
+            tables.append(table)
             if b % CODE_BLOCKS == 0:
                 pair = blocks.tile([P, CODE_BLOCKS * T], F32, name="pair")
                 nc.sync.dma_start(pair[:], pos_rows[:, b * T : (b + CODE_BLOCKS) * T])
                 codes.extend(pair[:, k * T : (k + 1) * T] for k in range(CODE_BLOCKS))
-            table = blocks.tile([P, S], F32, name="table")
-            nc.sync.dma_start(table[:], embedding_blocks[:, b, :])
-            tables.append(table)
+            if b == 0:
+                offsets = held.tile([P, N // 16], U16, name="offsets")
+                nc.sync.dma_start(offsets[:], offs)
 
         first = 0
         for g, size in enumerate(STORE_SEQUENCES):

@@ -6,7 +6,7 @@ T, N = 256, 1024
 BLOCKS = C // P
 SEQUENCES = N // T
 SEQ_COLS = T // 16
-CODE_BLOCKS = 2
+CODE_LOADS = (0, 2)
 STORE_SEQUENCES = (12, 8, 2, 2)
 F32, U16 = mybir.dt.float32, mybir.dt.uint16
 ADD = mybir.AluOpType.add
@@ -14,7 +14,7 @@ ADD = mybir.AluOpType.add
 
 def tile_microgpttorch_kernel(tc, embedding, pos, offs, out):
     nc = tc.nc
-    assert sum(STORE_SEQUENCES) == BLOCKS * SEQUENCES and BLOCKS % CODE_BLOCKS == 0
+    assert sum(STORE_SEQUENCES) == BLOCKS * SEQUENCES
     embedding_blocks = embedding.rearrange("(p b) s -> p b s", b=BLOCKS)
     pos_rows = pos.rearrange("(p b) t -> p (b t)", b=BLOCKS)
     out_rows = out.rearrange("(p b) n -> p (b n)", b=BLOCKS)
@@ -27,10 +27,11 @@ def tile_microgpttorch_kernel(tc, embedding, pos, offs, out):
             table = blocks.tile([P, S], F32, name="table")
             nc.sync.dma_start(table[:], embedding_blocks[:, b, :])
             tables.append(table)
-            if b % CODE_BLOCKS == 0:
-                pair = blocks.tile([P, CODE_BLOCKS * T], F32, name="pair")
-                nc.sync.dma_start(pair[:], pos_rows[:, b * T : (b + CODE_BLOCKS) * T])
-                codes.extend(pair[:, k * T : (k + 1) * T] for k in range(CODE_BLOCKS))
+            if b in CODE_LOADS:
+                end = min([c for c in CODE_LOADS if c > b] + [BLOCKS])
+                code = held.tile([P, (end - b) * T], F32, name="code%d" % b)
+                nc.sync.dma_start(code[:], pos_rows[:, b * T : end * T])
+                codes.extend(code[:, k * T : (k + 1) * T] for k in range(end - b))
             if b == 0:
                 offsets = held.tile([P, N // 16], U16, name="offsets")
                 nc.sync.dma_start(offsets[:], offs)

import concourse.mybir as mybir

P = 128
C, S = 768, 2048
T, N = 256, 1024
BLOCKS = C // P
SEQUENCES = N // T
SEQ_COLS = T // 16
CODE_LOADS = (0, 2)
STORE_SEQUENCES = (12, 8, 2, 2)
F32, U16 = mybir.dt.float32, mybir.dt.uint16
ADD = mybir.AluOpType.add


def tile_microgpttorch_kernel(tc, embedding, pos, offs, out):
    nc = tc.nc
    assert sum(STORE_SEQUENCES) == BLOCKS * SEQUENCES
    embedding_blocks = embedding.rearrange("(p b) s -> p b s", b=BLOCKS)
    pos_rows = pos.rearrange("(p b) t -> p (b t)", b=BLOCKS)
    out_rows = out.rearrange("(p b) n -> p (b n)", b=BLOCKS)
    with (
        tc.tile_pool(name="held", bufs=1) as held,
        tc.tile_pool(name="blocks", bufs=BLOCKS) as blocks,
    ):
        tables, codes = [], []
        for b in range(BLOCKS):
            table = blocks.tile([P, S], F32, name="table")
            nc.sync.dma_start(table[:], embedding_blocks[:, b, :])
            tables.append(table)
            if b in CODE_LOADS:
                end = min([c for c in CODE_LOADS if c > b] + [BLOCKS])
                code = held.tile([P, (end - b) * T], F32, name="code%d" % b)
                nc.sync.dma_start(code[:], pos_rows[:, b * T : end * T])
                codes.extend(code[:, k * T : (k + 1) * T] for k in range(end - b))
            if b == 0:
                offsets = held.tile([P, N // 16], U16, name="offsets")
                nc.sync.dma_start(offsets[:], offs)

        first = 0
        for g, size in enumerate(STORE_SEQUENCES):
            summed = held.tile([P, size * T], F32, name="summed%d" % g)
            for k in range(size):
                b, s = divmod(first + k, SEQUENCES)
                picked = tables[b][:].indirect(offsets[:, s * SEQ_COLS : (s + 1) * SEQ_COLS])
                nc.vector.tensor_tensor(summed[:, k * T : (k + 1) * T], picked, codes[b], ADD)
            nc.sync.dma_start(out_rows[:, first * T : (first + size) * T], summed[:])
            first += size
